import numpy as np
import ml_dtypes


def mxq(x, axis, fmt="e4m3"):
    dtype, down = {"e4m3": (ml_dtypes.float8_e4m3fn, 7), "e5m2": (ml_dtypes.float8_e5m2, 14)}[fmt]
    v = np.moveaxis(np.asarray(x, np.float32).astype(ml_dtypes.bfloat16).astype(np.float64), axis, -1)
    blocks = v.reshape(v.shape[:-1] + (-1, 32))
    amax = np.abs(blocks).max(-1, keepdims=True)
    byte = np.maximum(np.where(amax > 0, np.frexp(amax)[1] - 1 + 127, 0) - down, 1)
    scale = np.exp2(byte - 127.0)
    codes = (blocks / scale).astype(np.float32).astype(dtype).astype(np.float64)
    return np.moveaxis((codes * scale).reshape(v.shape), -1, axis)


WIDE = False


def mx_kscale(k):
    if not WIDE:
        return np.ones(k)
    levels = np.array([10, -10, 5, -5, 0])
    a = np.random.permutation(np.resize(levels, k // 512 * 4)).reshape(k // 512, 4)
    idx = np.arange(k)
    return np.exp2(a[idx // 512, idx % 128 // 32])


BF16 = ml_dtypes.bfloat16


def bf(x):
    return np.asarray(x, np.float32).astype(BF16)


def f64(x):
    return np.asarray(x).astype(np.float64)


B, S, D, P, PW, L = 2, 256, 1024, 4, 2, 2


def sigmoid(v):
    return 1.0 / (1.0 + np.exp(-v))


def setup_inputs():
    n = np.random.standard_normal
    s = mx_kscale(D)
    return {"x": bf(n((B, S, D)) * s),
            "amp_w": bf(n((D, D)) / np.sqrt(D) / s[:, None]),
            "amp_b": bf(n(D) * 0.3),
            "ph_w": bf(n((D, D)) / np.sqrt(D) / s[:, None]),
            "ph_b": bf(n(D) * 0.3)}


def reference(x, amp_w, amp_b, ph_w, ph_b):
    xq = mxq(f64(x), 2, "e4m3")
    amp = sigmoid((xq @ mxq(f64(amp_w), 0, "e4m3")) + f64(amp_b))
    ph = np.tanh((xq @ mxq(f64(ph_w), 0, "e4m3")) + f64(ph_b)) * np.pi
    return (np.cos(ph) + np.sin(ph)) * amp

@@ -1,0 +1,211 @@
+import math
+from contextlib import ExitStack
+
+import concourse.mybir as mybir
+from concourse.masks import make_identity
+
+BF16 = mybir.dt.bfloat16
+F32 = mybir.dt.float32
+U32 = mybir.dt.uint32
+U8 = mybir.dt.uint8
+FP8X4 = mybir.dt.float8_e4m3fn_x4
+ACT = mybir.ActivationFunctionType
+ALU = mybir.AluOpType
+
+P = 128
+PACK = 4
+K_PASS = P * PACK
+TOKENS = 512
+K = 1024
+FEATURES = 1024
+PASSES = K // K_PASS
+TOKEN_TILES = TOKENS // P
+FEATURE_TILES = FEATURES // P
+CHUNK = 256
+CHUNKS = FEATURES // CHUNK
+TILES_PER_CHUNK = CHUNK // P
+
+FLOPS = 2 * TOKENS * K * 2 * FEATURES
+
+
+def tile_quantuminspiredneuralcore_pa_kernel(tc, x, amp_w, amp_b, ph_w, ph_b, out):
+    nc = tc.nc
+    x_rows_dram = x.flatten_outer_dims()
+    weights_dram = {
+        "ph": ph_w.rearrange("(g p t) n -> g p t n", g=PASSES, t=PACK),
+        "amp": amp_w.rearrange("(g p t) n -> g p t n", g=PASSES, t=PACK),
+    }
+    out_dram = out.flatten_outer_dims().rearrange("(i p) f -> p i f", p=P)
+
+    with ExitStack() as ctx:
+        ctx.enter_context(tc.manual_schedule())
+        keep = ctx.enter_context(tc.tile_pool(name="keep", bufs=1))
+        raw_pool = ctx.enter_context(tc.tile_pool(name="raw", bufs=2 * CHUNKS))
+        grouped_pool = ctx.enter_context(tc.tile_pool(name="grouped", bufs=3))
+        quantised = ctx.enter_context(tc.tile_pool(name="quantised", bufs=2 * CHUNKS))
+        short = ctx.enter_context(tc.tile_pool(name="short", bufs=3))
+        long = ctx.enter_context(tc.tile_pool(name="long", bufs=FEATURE_TILES))
+        psum_t = ctx.enter_context(tc.psum_pool(name="psum_t", bufs=3))
+        psum_z = ctx.enter_context(tc.psum_pool(name="psum_z", bufs=5))
+
+        ident_f32 = keep.tile([P, P], F32)
+        make_identity(nc, ident_f32[:])
+        ident_bf16 = keep.tile([P, P], BF16)
+        make_identity(nc, ident_bf16[:])
+        neg_quarter = keep.tile([P, 1], F32)
+        nc.vector.memset(neg_quarter[:], -0.25)
+        half = keep.tile([P, 1], F32)
+        nc.vector.memset(half[:], 0.5)
+        half_pi = keep.tile([P, 1], F32)
+        nc.vector.tensor_scalar(out=half_pi[:], in0=half[:], scalar1=math.pi, scalar2=None, op0=ALU.mult)
+        bias_rows = keep.tile([P, P], BF16)
+        nc.vector.memset(bias_rows[:], 0.0)
+
+        nc.scalar.dma_start(out=bias_rows[0:FEATURE_TILES, :], in_=amp_b.rearrange("(j f) -> j f", f=P))
+        nc.scalar.dma_start(
+            out=bias_rows[FEATURE_TILES : 2 * FEATURE_TILES, :], in_=ph_b.rearrange("(j f) -> j f", f=P)
+        )
+
+        warm = keep.tile([P, 1], F32)
+        nc.scalar.activation(out=warm[:], in_=half[:], func=ACT.Silu)
+
+        raw = {}
+
+        def load_weights(m, q):
+            raw_tile = raw_pool.tile([P, PASSES, PACK, CHUNK], BF16, name="raw_tile")
+            for g in range(PASSES):
+                nc.sync.dma_start(out=raw_tile[:, g], in_=weights_dram[m][g, :, :, q * CHUNK : (q + 1) * CHUNK])
+            raw[(m, q)] = raw_tile
+
+        load_weights("ph", 0)
+        x_rows = []
+        for i in range(TOKEN_TILES):
+            x_tile = keep.tile([P, K], BF16, name="x_tile%d" % i)
+            nc.sync.dma_start(out=x_tile[:], in_=x_rows_dram[i * P : (i + 1) * P, :])
+            x_rows.append(x_tile)
+        load_weights("amp", 0)
+        for q in range(1, CHUNKS):
+            load_weights("ph", q)
+            load_weights("amp", q)
+
+        w_codes = {}
+        w_scales = {}
+
+        def prepare_weights(m, q):
+            grouped = grouped_pool.tile([P, PASSES, CHUNK, PACK], BF16, name="grouped", align_bytes=64)
+            codes = quantised.tile([P, PASSES * CHUNK], U32, name="codes", align_bytes=64)
+            scales = quantised.tile([P, PASSES * CHUNK], U8, name="scales", align_bytes=64)
+            for g in range(PASSES):
+                nc.vector.tensor_copy(
+                    out=grouped[:, g].rearrange("p (c i) t -> p c t i", i=4),
+                    in_=raw[(m, q)][:, g].rearrange("p t (c i) -> p c t i", i=4),
+                )
+            for g in range(PASSES):
+                cols = slice(g * CHUNK, (g + 1) * CHUNK)
+                nc.vector.quantize_mx(
+                    out=codes[:, cols].bitcast(FP8X4),
+                    scales=scales[:, cols],
+                    in_=grouped[:, g].rearrange("p n t -> p (n t)"),
+                )
+            w_codes[(m, q)] = codes
+            w_scales[(m, q)] = scales
+
+        prepare_weights("ph", 0)
+
+        x_grouped = keep.tile([P, PASSES * TOKENS * PACK], BF16, align_bytes=64)
+        x_grouped_words = x_grouped[:].bitcast(F32).rearrange("p (g r u) -> p g r u", g=PASSES, u=2)
+        x_codes = keep.tile([P, PASSES * TOKENS], U32, align_bytes=64)
+        x_scales = keep.tile([P, PASSES * TOKENS], U8, align_bytes=64)
+        for i in range(TOKEN_TILES):
+            words = x_rows[i][:].bitcast(F32).rearrange("r (g p u) -> r g u p", g=PASSES, u=2)
+            x_t = psum_t.tile([P, PASSES, 2, P], F32, name="x_t", tag="t")
+            for g in range(PASSES):
+                for u in range(2):
+                    nc.tensor.transpose(out=x_t[:, g, u, :], in_=words[:, g, u, :], identity=ident_f32[:])
+            nc.scalar.copy(
+                out=x_grouped_words[:, :, i * P : (i + 1) * P, :], in_=x_t[:].rearrange("p g u r -> p g r u")
+            )
+            for g in range(PASSES):
+                first = g * TOKENS + i * P
+                nc.vector.quantize_mx(
+                    out=x_codes[:, first : first + P].bitcast(FP8X4),
+                    scales=x_scales[:, first : first + P],
+                    in_=x_grouped[:, first * PACK : (first + P) * PACK],
+                )
+
+        bias_ps = psum_t.tile([P, P], BF16, name="bias_ps", tag="t")
+        nc.tensor.transpose(out=bias_ps[:], in_=bias_rows[:], identity=ident_bf16[:])
+        amp_bias_half = keep.tile([P, FEATURE_TILES], F32)
+        nc.vector.tensor_scalar(
+            out=amp_bias_half[:], in0=bias_ps[:, 0:FEATURE_TILES], scalar1=0.5, scalar2=None, op0=ALU.mult
+        )
+        ph_bias = keep.tile([P, FEATURE_TILES], F32)
+        nc.vector.tensor_copy(out=ph_bias[:], in_=bias_ps[:, FEATURE_TILES : 2 * FEATURE_TILES])
+
+        prepare_weights("amp", 0)
+        for q in range(1, CHUNKS):
+            prepare_weights("ph", q)
+            prepare_weights("amp", q)
+
+        def multiply(m, j):
+            q, jj = divmod(j, TILES_PER_CHUNK)
+            z = psum_z.tile([P, TOKENS], F32, name="z")
+            for g in range(PASSES):
+                w_cols = slice(g * CHUNK + jj * P, g * CHUNK + (jj + 1) * P)
+                x_cols = slice(g * TOKENS, (g + 1) * TOKENS)
+                nc.tensor.matmul_mx(
+                    out=z[:],
+                    lhsT=w_codes[(m, q)][:, w_cols].bitcast(FP8X4),
+                    lhsT_scale=w_scales[(m, q)][:, w_cols],
+                    rhs=x_codes[:, x_cols].bitcast(FP8X4),
+                    rhs_scale=x_scales[:, x_cols],
+                    start=(g == 0),
+                    stop=(g == PASSES - 1),
+                )
+            return z
+
+        amp_tanh = {}
+        sine = {}
+        for q in range(CHUNKS):
+            tiles = range(q * TILES_PER_CHUNK, (q + 1) * TILES_PER_CHUNK)
+            z_ph = {}
+            z_amp = {}
+            tanh_ph = {}
+            folded = {}
+            for j in tiles:
+                z_ph[j] = multiply("ph", j)
+            for j in tiles:
+                z_amp[j] = multiply("amp", j)
+            for j in tiles:
+                tanh_ph[j] = short.tile([P, TOKENS], F32, name="tanh_ph")
+                nc.scalar.activation(out=tanh_ph[j][:], in_=z_ph[j][:], func=ACT.Tanh, bias=ph_bias[:, j : j + 1], scale=1.0)
+            for j in tiles:
+                folded[j] = short.tile([P, TOKENS], F32, name="folded")
+                nc.scalar.activation(out=folded[j][:], in_=tanh_ph[j][:], func=ACT.Abs, bias=neg_quarter[:, 0:1], scale=1.0)
+            for j in tiles:
+                amp_tanh[j] = long.tile([P, TOKENS], F32, name="amp_tanh")
+                nc.scalar.activation(
+                    out=amp_tanh[j][:], in_=z_amp[j][:], func=ACT.Tanh, bias=amp_bias_half[:, j : j + 1], scale=0.5
+                )
+            for j in tiles:
+                sine[j] = long.tile([P, TOKENS], F32, name="sine")
+                nc.scalar.activation(out=sine[j][:], in_=folded[j][:], func=ACT.Sin, bias=half_pi[:, 0:1], scale=-math.pi)
+
+        transposed = {}
+        for j in range(FEATURE_TILES + 1):
+            if j < FEATURE_TILES:
+                product = short.tile([P, TOKENS], F32, name="product")
+                nc.vector.scalar_tensor_tensor(
+                    out=product[:], in0=amp_tanh[j][:], scalar=1.0, in1=sine[j][:], op0=ALU.add, op1=ALU.mult
+                )
+                transposed[j] = psum_t.tile([P, TOKEN_TILES, P], F32, name="transposed", tag="t")
+                for i in range(TOKEN_TILES):
+                    nc.tensor.transpose(
+                        out=transposed[j][:, i, :], in_=product[:, i * P : (i + 1) * P], identity=ident_f32[:]
+                    )
+            if j > 0:
+                result = short.tile([P, TOKEN_TILES, P], F32, name="result")
+                nc.vector.tensor_scalar(
+                    out=result[:], in0=transposed[j - 1][:], scalar1=math.sqrt(0.5), scalar2=None, op0=ALU.mult
+                )
+                nc.sync.dma_start(out=out_dram[:, :, (j - 1) * P : j * P], in_=result[:])

@@ -191,9 +191,10 @@ def tile_quantuminspiredneuralcore_pa_kernel(tc, x, amp_w, amp_b, ph_w, ph_b, ou
                 sine[j] = long.tile([P, TOKENS], F32, name="sine")
                 nc.scalar.activation(out=sine[j][:], in_=folded[j][:], func=ACT.Sin, bias=half_pi[:, 0:1], scale=-math.pi)
 
-        transposed = {}
-        for j in range(FEATURE_TILES + 1):
-            if j < FEATURE_TILES:
+        for q in range(CHUNKS):
+            tiles = range(q * TILES_PER_CHUNK, (q + 1) * TILES_PER_CHUNK)
+            transposed = {}
+            for j in tiles:
                 product = short.tile([P, TOKENS], F32, name="product")
                 nc.vector.scalar_tensor_tensor(
                     out=product[:], in0=amp_tanh[j][:], scalar=1.0, in1=sine[j][:], op0=ALU.add, op1=ALU.mult
@@ -203,9 +204,9 @@ def tile_quantuminspiredneuralcore_pa_kernel(tc, x, amp_w, amp_b, ph_w, ph_b, ou
                     nc.tensor.transpose(
                         out=transposed[j][:, i, :], in_=product[:, i * P : (i + 1) * P], identity=ident_f32[:]
                     )
-            if j > 0:
-                result = short.tile([P, TOKEN_TILES, P], F32, name="result")
+            for j in tiles:
+                result = long.tile([P, TOKEN_TILES, P], F32, name="result")
                 nc.vector.tensor_scalar(
-                    out=result[:], in0=transposed[j - 1][:], scalar1=math.sqrt(0.5), scalar2=None, op0=ALU.mult
+                    out=result[:], in0=transposed[j][:], scalar1=math.sqrt(0.5), scalar2=None, op0=ALU.mult
                 )
-                nc.sync.dma_start(out=out_dram[:, :, (j - 1) * P : j * P], in_=result[:])
+                nc.sync.dma_start(out=out_dram[:, :, j * P : (j + 1) * P], in_=result[:])

@@ -43,10 +43,10 @@ def tile_quantuminspiredneuralcore_pa_kernel(tc, x, amp_w, amp_b, ph_w, ph_b, ou
         raw_pool = ctx.enter_context(tc.tile_pool(name="raw", bufs=2 * CHUNKS))
         grouped_pool = ctx.enter_context(tc.tile_pool(name="grouped", bufs=3))
         quantised = ctx.enter_context(tc.tile_pool(name="quantised", bufs=2 * CHUNKS))
-        short = ctx.enter_context(tc.tile_pool(name="short", bufs=3))
-        long = ctx.enter_context(tc.tile_pool(name="long", bufs=FEATURE_TILES))
-        psum_t = ctx.enter_context(tc.psum_pool(name="psum_t", bufs=3))
-        psum_z = ctx.enter_context(tc.psum_pool(name="psum_z", bufs=5))
+        work = ctx.enter_context(tc.tile_pool(name="work", bufs=3 * TILES_PER_CHUNK))
+        results = ctx.enter_context(tc.tile_pool(name="results", bufs=FEATURE_TILES))
+        psum_z = ctx.enter_context(tc.psum_pool(name="psum_z", bufs=2 * TILES_PER_CHUNK))
+        psum_turned = ctx.enter_context(tc.psum_pool(name="psum_turned", bufs=TILES_PER_CHUNK))
 
         ident_f32 = keep.tile([P, P], F32)
         make_identity(nc, ident_f32[:])
@@ -110,6 +110,77 @@ def tile_quantuminspiredneuralcore_pa_kernel(tc, x, amp_w, amp_b, ph_w, ph_b, ou
             w_codes[(m, q)] = codes
             w_scales[(m, q)] = scales
 
+        def tiles_of(q):
+            return range(q * TILES_PER_CHUNK, (q + 1) * TILES_PER_CHUNK)
+
+        z = {}
+
+        def multiply(m, q):
+            for jj, j in enumerate(tiles_of(q)):
+                z[(m, j)] = psum_z.tile([P, TOKENS], F32, name="z")
+                for g in range(PASSES):
+                    w_cols = slice(g * CHUNK + jj * P, g * CHUNK + (jj + 1) * P)
+                    x_cols = slice(g * TOKENS, (g + 1) * TOKENS)
+                    nc.tensor.matmul_mx(
+                        out=z[(m, j)][:],
+                        lhsT=w_codes[(m, q)][:, w_cols].bitcast(FP8X4),
+                        lhsT_scale=w_scales[(m, q)][:, w_cols],
+                        rhs=x_codes[:, x_cols].bitcast(FP8X4),
+                        rhs_scale=x_scales[:, x_cols],
+                        start=(g == 0),
+                        stop=(g == PASSES - 1),
+                    )
+
+        def turn(source, tag):
+            turned = psum_turned.tile([P, TOKEN_TILES, P], F32, name="turned", tag=tag)
+            for i in range(TOKEN_TILES):
+                nc.tensor.transpose(out=turned[:, i, :], in_=source[:, i * P : (i + 1) * P], identity=ident_f32[:])
+            return turned
+
+        tanh_ph = {}
+        tanh_amp = {}
+        tanh_ph_turned = {}
+        amp_turned = {}
+        sine = {}
+
+        def squash(q):
+            for j in tiles_of(q):
+                tanh_ph[j] = work.tile([P, TOKENS], F32, name="tanh_ph")
+                nc.scalar.activation(
+                    out=tanh_ph[j][:], in_=z[("ph", j)][:], func=ACT.Tanh, bias=ph_bias[:, j : j + 1], scale=1.0
+                )
+            for j in tiles_of(q):
+                tanh_amp[j] = work.tile([P, TOKENS], F32, name="tanh_amp")
+                nc.scalar.activation(
+                    out=tanh_amp[j][:], in_=z[("amp", j)][:], func=ACT.Tanh, bias=amp_bias_half[:, j : j + 1], scale=0.5
+                )
+
+        def wave(q):
+            folded = {}
+            for j in tiles_of(q):
+                folded[j] = work.tile([P, TOKEN_TILES, P], F32, name="folded")
+                nc.scalar.activation(
+                    out=folded[j][:], in_=tanh_ph_turned[j][:], func=ACT.Abs, bias=neg_quarter[:, 0:1], scale=1.0
+                )
+            for j in tiles_of(q):
+                sine[j] = work.tile([P, TOKEN_TILES, P], F32, name="sine")
+                nc.scalar.activation(out=sine[j][:], in_=folded[j][:], func=ACT.Sin, bias=half_pi[:, 0:1], scale=-math.pi)
+
+        amp = {}
+
+        def scale_amp(q):
+            for j in tiles_of(q):
+                amp[j] = work.tile([P, TOKENS], F32, name="amp")
+                nc.vector.tensor_scalar(
+                    out=amp[j][:], in0=tanh_amp[j][:], scalar1=math.sqrt(0.5), scalar2=math.sqrt(0.5), op0=ALU.mult, op1=ALU.add
+                )
+
+        def finish(q):
+            for j in tiles_of(q):
+                result = results.tile([P, TOKEN_TILES, P], F32, name="result")
+                nc.vector.tensor_tensor(out=result[:], in0=amp_turned[j][:], in1=sine[j][:], op=ALU.mult)
+                nc.sync.dma_start(out=out_dram[:, :, j * P : (j + 1) * P], in_=result[:])
+
         prepare_weights("ph", 0)
 
         x_grouped = keep.tile([P, PASSES * TOKENS * PACK], BF16, align_bytes=64)
@@ -118,7 +189,7 @@ def tile_quantuminspiredneuralcore_pa_kernel(tc, x, amp_w, amp_b, ph_w, ph_b, ou
         x_scales = keep.tile([P, PASSES * TOKENS], U8, align_bytes=64)
         for i in range(TOKEN_TILES):
             words = x_rows[i][:].bitcast(F32).rearrange("r (g p u) -> r g u p", g=PASSES, u=2)
-            x_t = psum_t.tile([P, PASSES, 2, P], F32, name="x_t", tag="t")
+            x_t = psum_z.tile([P, PASSES, 2, P], F32, name="x_t", tag="z")
             for g in range(PASSES):
                 for u in range(2):
                     nc.tensor.transpose(out=x_t[:, g, u, :], in_=words[:, g, u, :], identity=ident_f32[:])
@@ -133,7 +204,7 @@ def tile_quantuminspiredneuralcore_pa_kernel(tc, x, amp_w, amp_b, ph_w, ph_b, ou
                     in_=x_grouped[:, first * PACK : (first + P) * PACK],
                 )
 
-        bias_ps = psum_t.tile([P, P], BF16, name="bias_ps", tag="t")
+        bias_ps = psum_turned.tile([P, P], BF16, name="bias_ps", tag="amp")
         nc.tensor.transpose(out=bias_ps[:], in_=bias_rows[:], identity=ident_bf16[:])
         amp_bias_half = keep.tile([P, FEATURE_TILES], F32)
         nc.vector.tensor_scalar(
@@ -143,70 +214,22 @@ def tile_quantuminspiredneuralcore_pa_kernel(tc, x, amp_w, amp_b, ph_w, ph_b, ou
         nc.vector.tensor_copy(out=ph_bias[:], in_=bias_ps[:, FEATURE_TILES : 2 * FEATURE_TILES])
 
         prepare_weights("amp", 0)
-        for q in range(1, CHUNKS):
-            prepare_weights("ph", q)
-            prepare_weights("amp", q)
 
-        def multiply(m, j):
-            q, jj = divmod(j, TILES_PER_CHUNK)
-            z = psum_z.tile([P, TOKENS], F32, name="z")
-            for g in range(PASSES):
-                w_cols = slice(g * CHUNK + jj * P, g * CHUNK + (jj + 1) * P)
-                x_cols = slice(g * TOKENS, (g + 1) * TOKENS)
-                nc.tensor.matmul_mx(
-                    out=z[:],
-                    lhsT=w_codes[(m, q)][:, w_cols].bitcast(FP8X4),
-                    lhsT_scale=w_scales[(m, q)][:, w_cols],
-                    rhs=x_codes[:, x_cols].bitcast(FP8X4),
-                    rhs_scale=x_scales[:, x_cols],
-                    start=(g == 0),
-                    stop=(g == PASSES - 1),
-                )
-            return z
-
-        amp_tanh = {}
-        sine = {}
-        for q in range(CHUNKS):
-            tiles = range(q * TILES_PER_CHUNK, (q + 1) * TILES_PER_CHUNK)
-            z_ph = {}
-            z_amp = {}
-            tanh_ph = {}
-            folded = {}
-            for j in tiles:
-                z_ph[j] = multiply("ph", j)
-            for j in tiles:
-                z_amp[j] = multiply("amp", j)
-            for j in tiles:
-                tanh_ph[j] = short.tile([P, TOKENS], F32, name="tanh_ph")
-                nc.scalar.activation(out=tanh_ph[j][:], in_=z_ph[j][:], func=ACT.Tanh, bias=ph_bias[:, j : j + 1], scale=1.0)
-            for j in tiles:
-                folded[j] = short.tile([P, TOKENS], F32, name="folded")
-                nc.scalar.activation(out=folded[j][:], in_=tanh_ph[j][:], func=ACT.Abs, bias=neg_quarter[:, 0:1], scale=1.0)
-            for j in tiles:
-                amp_tanh[j] = long.tile([P, TOKENS], F32, name="amp_tanh")
-                nc.scalar.activation(
-                    out=amp_tanh[j][:], in_=z_amp[j][:], func=ACT.Tanh, bias=amp_bias_half[:, j : j + 1], scale=0.5
-                )
-            for j in tiles:
-                sine[j] = long.tile([P, TOKENS], F32, name="sine")
-                nc.scalar.activation(out=sine[j][:], in_=folded[j][:], func=ACT.Sin, bias=half_pi[:, 0:1], scale=-math.pi)
-
-        for q in range(CHUNKS):
-            tiles = range(q * TILES_PER_CHUNK, (q + 1) * TILES_PER_CHUNK)
-            transposed = {}
-            for j in tiles:
-                product = short.tile([P, TOKENS], F32, name="product")
-                nc.vector.scalar_tensor_tensor(
-                    out=product[:], in0=amp_tanh[j][:], scalar=1.0, in1=sine[j][:], op0=ALU.add, op1=ALU.mult
-                )
-                transposed[j] = psum_t.tile([P, TOKEN_TILES, P], F32, name="transposed", tag="t")
-                for i in range(TOKEN_TILES):
-                    nc.tensor.transpose(
-                        out=transposed[j][:, i, :], in_=product[:, i * P : (i + 1) * P], identity=ident_f32[:]
-                    )
-            for j in tiles:
-                result = long.tile([P, TOKEN_TILES, P], F32, name="result")
-                nc.vector.tensor_scalar(
-                    out=result[:], in0=transposed[j][:], scalar1=math.sqrt(0.5), scalar2=None, op0=ALU.mult
-                )
-                nc.sync.dma_start(out=out_dram[:, :, j * P : (j + 1) * P], in_=result[:])
+        for k in range(CHUNKS + 1):
+            if k < CHUNKS:
+                multiply("ph", k)
+                multiply("amp", k)
+                squash(k)
+                for j in tiles_of(k):
+                    tanh_ph_turned[j] = turn(tanh_ph[j], "ph")
+                wave(k)
+            if k >= 1:
+                for j in tiles_of(k - 1):
+                    amp_turned[j] = turn(amp[j], "amp")
+            if k + 1 < CHUNKS:
+                prepare_weights("ph", k + 1)
+                prepare_weights("amp", k + 1)
+            if k < CHUNKS:
+                scale_amp(k)
+            if k >= 1:
+                finish(k - 1)

@@ -58,6 +58,8 @@ def tile_quantuminspiredneuralcore_pa_kernel(tc, x, amp_w, amp_b, ph_w, ph_b, ou
         nc.vector.memset(half[:], 0.5)
         half_pi = keep.tile([P, 1], F32)
         nc.vector.tensor_scalar(out=half_pi[:], in0=half[:], scalar1=math.pi, scalar2=None, op0=ALU.mult)
+        ones_f32 = keep.tile([P, P], F32)
+        nc.vector.memset(ones_f32[:], 1.0)
         bias_rows = keep.tile([P, P], BF16)
         nc.vector.memset(bias_rows[:], 0.0)
 
@@ -137,6 +139,22 @@ def tile_quantuminspiredneuralcore_pa_kernel(tc, x, amp_w, amp_b, ph_w, ph_b, ou
                 nc.tensor.transpose(out=turned[:, i, :], in_=source[:, i * P : (i + 1) * P], identity=ident_f32[:])
             return turned
 
+        def turn_plus_one(source, tag):
+            turned = psum_turned.tile([P, TOKEN_TILES, P], F32, name="turned", tag=tag)
+            for i in range(TOKEN_TILES):
+                nc.tensor.matmul(
+                    out=turned[:, i, :], lhsT=ones_f32[:], rhs=ident_f32[:], is_transpose=True, start=True, stop=False
+                )
+                nc.tensor.matmul(
+                    out=turned[:, i, :],
+                    lhsT=source[:, i * P : (i + 1) * P],
+                    rhs=ident_f32[:],
+                    is_transpose=True,
+                    start=False,
+                    stop=True,
+                )
+            return turned
+
         tanh_ph = {}
         tanh_amp = {}
         tanh_ph_turned = {}
@@ -166,19 +184,12 @@ def tile_quantuminspiredneuralcore_pa_kernel(tc, x, amp_w, amp_b, ph_w, ph_b, ou
                 sine[j] = work.tile([P, TOKEN_TILES, P], F32, name="sine")
                 nc.scalar.activation(out=sine[j][:], in_=folded[j][:], func=ACT.Sin, bias=half_pi[:, 0:1], scale=-math.pi)
 
-        amp = {}
-
-        def scale_amp(q):
-            for j in tiles_of(q):
-                amp[j] = work.tile([P, TOKENS], F32, name="amp")
-                nc.vector.tensor_scalar(
-                    out=amp[j][:], in0=tanh_amp[j][:], scalar1=math.sqrt(0.5), scalar2=math.sqrt(0.5), op0=ALU.mult, op1=ALU.add
-                )
-
         def finish(q):
             for j in tiles_of(q):
                 result = results.tile([P, TOKEN_TILES, P], F32, name="result")
-                nc.vector.tensor_tensor(out=result[:], in0=amp_turned[j][:], in1=sine[j][:], op=ALU.mult)
+                nc.vector.scalar_tensor_tensor(
+                    out=result[:], in0=amp_turned[j][:], scalar=math.sqrt(0.5), in1=sine[j][:], op0=ALU.mult, op1=ALU.mult
+                )
                 nc.sync.dma_start(out=out_dram[:, :, j * P : (j + 1) * P], in_=result[:])
 
         prepare_weights("ph", 0)
@@ -225,11 +236,9 @@ def tile_quantuminspiredneuralcore_pa_kernel(tc, x, amp_w, amp_b, ph_w, ph_b, ou
                 wave(k)
             if k >= 1:
                 for j in tiles_of(k - 1):
-                    amp_turned[j] = turn(amp[j], "amp")
+                    amp_turned[j] = turn_plus_one(tanh_amp[j], "amp")
             if k + 1 < CHUNKS:
                 prepare_weights("ph", k + 1)
                 prepare_weights("amp", k + 1)
-            if k < CHUNKS:
-                scale_amp(k)
             if k >= 1:
                 finish(k - 1)

@@ -25,6 +25,8 @@ CHUNK = 256
 CHUNKS = FEATURES // CHUNK
 TILES_PER_CHUNK = CHUNK // P
 
+HALF_ANGLE_TILES = (1, 3)
+
 FLOPS = 2 * TOKENS * K * 2 * FEATURES
 
 
@@ -60,6 +62,8 @@ def tile_quantuminspiredneuralcore_pa_kernel(tc, x, amp_w, amp_b, ph_w, ph_b, ou
         nc.vector.tensor_scalar(out=half_pi[:], in0=half[:], scalar1=math.pi, scalar2=None, op0=ALU.mult)
         ones_f32 = keep.tile([P, P], F32)
         nc.vector.memset(ones_f32[:], 1.0)
+        eighth_pi = keep.tile([P, 1], F32)
+        nc.vector.tensor_scalar(out=eighth_pi[:], in0=half[:], scalar1=math.pi / 4.0, scalar2=None, op0=ALU.mult)
         bias_rows = keep.tile([P, P], BF16)
         nc.vector.memset(bias_rows[:], 0.0)
 
@@ -139,8 +143,8 @@ def tile_quantuminspiredneuralcore_pa_kernel(tc, x, amp_w, amp_b, ph_w, ph_b, ou
                 nc.tensor.transpose(out=turned[:, i, :], in_=source[:, i * P : (i + 1) * P], identity=ident_f32[:])
             return turned
 
-        def turn_plus_one(source, tag):
-            turned = psum_turned.tile([P, TOKEN_TILES, P], F32, name="turned", tag=tag)
+        def turn_plus_one(source, pool, tag):
+            turned = pool.tile([P, TOKEN_TILES, P], F32, name="turned", tag=tag)
             for i in range(TOKEN_TILES):
                 nc.tensor.matmul(
                     out=turned[:, i, :], lhsT=ones_f32[:], rhs=ident_f32[:], is_transpose=True, start=True, stop=False
@@ -176,20 +180,38 @@ def tile_quantuminspiredneuralcore_pa_kernel(tc, x, amp_w, amp_b, ph_w, ph_b, ou
         def wave(q):
             folded = {}
             for j in tiles_of(q):
-                folded[j] = work.tile([P, TOKEN_TILES, P], F32, name="folded")
-                nc.scalar.activation(
-                    out=folded[j][:], in_=tanh_ph_turned[j][:], func=ACT.Abs, bias=neg_quarter[:, 0:1], scale=1.0
-                )
+                if j in HALF_ANGLE_TILES:
+                    sine[j] = work.tile([P, TOKEN_TILES, P], F32, name="sine")
+                    nc.scalar.activation(
+                        out=sine[j][:], in_=tanh_ph_turned[j][:], func=ACT.Sin, bias=eighth_pi[:, 0:1], scale=-math.pi / 2.0
+                    )
+                else:
+                    folded[j] = work.tile([P, TOKEN_TILES, P], F32, name="folded")
+                    nc.scalar.activation(
+                        out=folded[j][:], in_=tanh_ph_turned[j][:], func=ACT.Abs, bias=neg_quarter[:, 0:1], scale=1.0
+                    )
             for j in tiles_of(q):
-                sine[j] = work.tile([P, TOKEN_TILES, P], F32, name="sine")
-                nc.scalar.activation(out=sine[j][:], in_=folded[j][:], func=ACT.Sin, bias=half_pi[:, 0:1], scale=-math.pi)
+                if j not in HALF_ANGLE_TILES:
+                    sine[j] = work.tile([P, TOKEN_TILES, P], F32, name="sine")
+                    nc.scalar.activation(
+                        out=sine[j][:], in_=folded[j][:], func=ACT.Sin, bias=half_pi[:, 0:1], scale=-math.pi
+                    )
 
         def finish(q):
             for j in tiles_of(q):
                 result = results.tile([P, TOKEN_TILES, P], F32, name="result")
-                nc.vector.scalar_tensor_tensor(
-                    out=result[:], in0=amp_turned[j][:], scalar=math.sqrt(0.5), in1=sine[j][:], op0=ALU.mult, op1=ALU.mult
-                )
+                if j in HALF_ANGLE_TILES:
+                    scaled_square = work.tile([P, TOKEN_TILES, P], F32, name="scaled_square")
+                    nc.vector.scalar_tensor_tensor(
+                        out=scaled_square[:], in0=sine[j][:], scalar=-math.sqrt(2.0), in1=sine[j][:], op0=ALU.mult, op1=ALU.mult
+                    )
+                    nc.vector.scalar_tensor_tensor(
+                        out=result[:], in0=scaled_square[:], scalar=math.sqrt(0.5), in1=amp_turned[j][:], op0=ALU.add, op1=ALU.mult
+                    )
+                else:
+                    nc.vector.scalar_tensor_tensor(
+                        out=result[:], in0=amp_turned[j][:], scalar=math.sqrt(0.5), in1=sine[j][:], op0=ALU.mult, op1=ALU.mult
+                    )
                 nc.sync.dma_start(out=out_dram[:, :, j * P : (j + 1) * P], in_=result[:])
 
         prepare_weights("ph", 0)
@@ -236,7 +258,10 @@ def tile_quantuminspiredneuralcore_pa_kernel(tc, x, amp_w, amp_b, ph_w, ph_b, ou
                 wave(k)
             if k >= 1:
                 for j in tiles_of(k - 1):
-                    amp_turned[j] = turn_plus_one(tanh_amp[j], "amp")
+                    if k == CHUNKS:
+                        amp_turned[j] = turn_plus_one(tanh_amp[j], psum_z, "z")
+                    else:
+                        amp_turned[j] = turn_plus_one(tanh_amp[j], psum_turned, "amp")
             if k + 1 < CHUNKS:
                 prepare_weights("ph", k + 1)
                 prepare_weights("amp", k + 1)

@@ -25,7 +25,7 @@ CHUNK = 256
 CHUNKS = FEATURES // CHUNK
 TILES_PER_CHUNK = CHUNK // P
 
-HALF_ANGLE_TILES = (1, 3)
+HALF_ANGLE_TILES = (1, 3, 5)
 
 FLOPS = 2 * TOKENS * K * 2 * FEATURES
 
@@ -97,15 +97,21 @@ def tile_quantuminspiredneuralcore_pa_kernel(tc, x, amp_w, amp_b, ph_w, ph_b, ou
         w_codes = {}
         w_scales = {}
 
-        def prepare_weights(m, q):
+        def prepare_weights(m, q, scalar_passes=()):
             grouped = grouped_pool.tile([P, PASSES, CHUNK, PACK], BF16, name="grouped", align_bytes=64)
             codes = quantised.tile([P, PASSES * CHUNK], U32, name="codes", align_bytes=64)
             scales = quantised.tile([P, PASSES * CHUNK], U8, name="scales", align_bytes=64)
             for g in range(PASSES):
-                nc.vector.tensor_copy(
-                    out=grouped[:, g].rearrange("p (c i) t -> p c t i", i=4),
-                    in_=raw[(m, q)][:, g].rearrange("p t (c i) -> p c t i", i=4),
-                )
+                if g in scalar_passes:
+                    nc.scalar.copy(
+                        out=grouped[:, g].rearrange("p (c i) t -> p c t i", i=4),
+                        in_=raw[(m, q)][:, g].rearrange("p t (c i) -> p c t i", i=4),
+                    )
+                else:
+                    nc.vector.tensor_copy(
+                        out=grouped[:, g].rearrange("p (c i) t -> p c t i", i=4),
+                        in_=raw[(m, q)][:, g].rearrange("p t (c i) -> p c t i", i=4),
+                    )
             for g in range(PASSES):
                 cols = slice(g * CHUNK, (g + 1) * CHUNK)
                 nc.vector.quantize_mx(
@@ -198,15 +204,18 @@ def tile_quantuminspiredneuralcore_pa_kernel(tc, x, amp_w, amp_b, ph_w, ph_b, ou
                     )
 
         def finish(q):
+            scaled_square = {}
+            for j in tiles_of(q):
+                if j in HALF_ANGLE_TILES:
+                    scaled_square[j] = work.tile([P, TOKEN_TILES, P], F32, name="scaled_square")
+                    nc.vector.scalar_tensor_tensor(
+                        out=scaled_square[j][:], in0=sine[j][:], scalar=-math.sqrt(2.0), in1=sine[j][:], op0=ALU.mult, op1=ALU.mult
+                    )
             for j in tiles_of(q):
                 result = results.tile([P, TOKEN_TILES, P], F32, name="result")
                 if j in HALF_ANGLE_TILES:
-                    scaled_square = work.tile([P, TOKEN_TILES, P], F32, name="scaled_square")
                     nc.vector.scalar_tensor_tensor(
-                        out=scaled_square[:], in0=sine[j][:], scalar=-math.sqrt(2.0), in1=sine[j][:], op0=ALU.mult, op1=ALU.mult
-                    )
-                    nc.vector.scalar_tensor_tensor(
-                        out=result[:], in0=scaled_square[:], scalar=math.sqrt(0.5), in1=amp_turned[j][:], op0=ALU.add, op1=ALU.mult
+                        out=result[:], in0=scaled_square[j][:], scalar=math.sqrt(0.5), in1=amp_turned[j][:], op0=ALU.add, op1=ALU.mult
                     )
                 else:
                     nc.vector.scalar_tensor_tensor(
@@ -214,10 +223,8 @@ def tile_quantuminspiredneuralcore_pa_kernel(tc, x, amp_w, amp_b, ph_w, ph_b, ou
                     )
                 nc.sync.dma_start(out=out_dram[:, :, j * P : (j + 1) * P], in_=result[:])
 
-        prepare_weights("ph", 0)
+        prepare_weights("ph", 0, scalar_passes=(1,))
 
-        x_grouped = keep.tile([P, PASSES * TOKENS * PACK], BF16, align_bytes=64)
-        x_grouped_words = x_grouped[:].bitcast(F32).rearrange("p (g r u) -> p g r u", g=PASSES, u=2)
         x_codes = keep.tile([P, PASSES * TOKENS], U32, align_bytes=64)
         x_scales = keep.tile([P, PASSES * TOKENS], U8, align_bytes=64)
         for i in range(TOKEN_TILES):
@@ -226,15 +233,17 @@ def tile_quantuminspiredneuralcore_pa_kernel(tc, x, amp_w, amp_b, ph_w, ph_b, ou
             for g in range(PASSES):
                 for u in range(2):
                     nc.tensor.transpose(out=x_t[:, g, u, :], in_=words[:, g, u, :], identity=ident_f32[:])
+            x_grouped = keep.tile([P, PASSES * P * PACK], BF16, name="x_grouped%d" % i, align_bytes=64)
             nc.scalar.copy(
-                out=x_grouped_words[:, :, i * P : (i + 1) * P, :], in_=x_t[:].rearrange("p g u r -> p g r u")
+                out=x_grouped[:].bitcast(F32).rearrange("p (g r u) -> p g r u", g=PASSES, u=2),
+                in_=x_t[:].rearrange("p g u r -> p g r u"),
             )
             for g in range(PASSES):
                 first = g * TOKENS + i * P
                 nc.vector.quantize_mx(
                     out=x_codes[:, first : first + P].bitcast(FP8X4),
                     scales=x_scales[:, first : first + P],
-                    in_=x_grouped[:, first * PACK : (first + P) * PACK],
+                    in_=x_grouped[:, g * P * PACK : (g + 1) * P * PACK],
                 )
 
         bias_ps = psum_turned.tile([P, P], BF16, name="bias_ps", tag="amp")
@@ -246,7 +255,7 @@ def tile_quantuminspiredneuralcore_pa_kernel(tc, x, amp_w, amp_b, ph_w, ph_b, ou
         ph_bias = keep.tile([P, FEATURE_TILES], F32)
         nc.vector.tensor_copy(out=ph_bias[:], in_=bias_ps[:, FEATURE_TILES : 2 * FEATURE_TILES])
 
-        prepare_weights("amp", 0)
+        prepare_weights("amp", 0, scalar_passes=(1,))
 
         for k in range(CHUNKS + 1):
             if k < CHUNKS:

@@ -27,6 +27,9 @@ TILES_PER_CHUNK = CHUNK // P
 
 HALF_ANGLE_TILES = (1, 3, 5)
 
+WARM_UP_FIRST = 6
+WARM_UP_LAST = 2
+
 FLOPS = 2 * TOKENS * K * 2 * FEATURES
 
 
@@ -49,6 +52,16 @@ def tile_quantuminspiredneuralcore_pa_kernel(tc, x, amp_w, amp_b, ph_w, ph_b, ou
         results = ctx.enter_context(tc.tile_pool(name="results", bufs=FEATURE_TILES))
         psum_z = ctx.enter_context(tc.psum_pool(name="psum_z", bufs=2 * TILES_PER_CHUNK))
         psum_turned = ctx.enter_context(tc.psum_pool(name="psum_turned", bufs=TILES_PER_CHUNK))
+
+        idle_rows = keep.tile([P, TOKENS], BF16)
+        nc.vector.memset(idle_rows[:], 0.0)
+        idle_ps = psum_turned.tile([P, TOKENS], F32, name="idle_ps", tag="ph")
+
+        def keep_warm(count):
+            for n in range(count):
+                nc.tensor.matmul(out=idle_ps[:], lhsT=idle_rows[:, 0:P], rhs=idle_rows[:], start=True, stop=True)
+
+        keep_warm(WARM_UP_FIRST)
 
         ident_f32 = keep.tile([P, P], F32)
         make_identity(nc, ident_f32[:])
@@ -125,6 +138,11 @@ def tile_quantuminspiredneuralcore_pa_kernel(tc, x, amp_w, amp_b, ph_w, ph_b, ou
         def tiles_of(q):
             return range(q * TILES_PER_CHUNK, (q + 1) * TILES_PER_CHUNK)
 
+        def parts_of(j):
+            if j == FEATURE_TILES - 1:
+                return (slice(0, TOKEN_TILES // 2), slice(TOKEN_TILES // 2, TOKEN_TILES))
+            return (slice(0, TOKEN_TILES),)
+
         z = {}
 
         def multiply(m, q):
@@ -143,8 +161,8 @@ def tile_quantuminspiredneuralcore_pa_kernel(tc, x, amp_w, amp_b, ph_w, ph_b, ou
                         stop=(g == PASSES - 1),
                     )
 
-        def turn(source, tag):
-            turned = psum_turned.tile([P, TOKEN_TILES, P], F32, name="turned", tag=tag)
+        def turn(source, pool, tag):
+            turned = pool.tile([P, TOKEN_TILES, P], F32, name="turned", tag=tag)
             for i in range(TOKEN_TILES):
                 nc.tensor.transpose(out=turned[:, i, :], in_=source[:, i * P : (i + 1) * P], identity=ident_f32[:])
             return turned
@@ -199,9 +217,19 @@ def tile_quantuminspiredneuralcore_pa_kernel(tc, x, amp_w, amp_b, ph_w, ph_b, ou
             for j in tiles_of(q):
                 if j not in HALF_ANGLE_TILES:
                     sine[j] = work.tile([P, TOKEN_TILES, P], F32, name="sine")
-                    nc.scalar.activation(
-                        out=sine[j][:], in_=folded[j][:], func=ACT.Sin, bias=half_pi[:, 0:1], scale=-math.pi
-                    )
+                    for part in parts_of(j):
+                        nc.scalar.activation(
+                            out=sine[j][:, part, :], in_=folded[j][:, part, :], func=ACT.Sin, bias=half_pi[:, 0:1], scale=-math.pi
+                        )
+
+        amp = {}
+
+        def scale_amp(q):
+            for j in tiles_of(q):
+                amp[j] = work.tile([P, TOKENS], F32, name="amp")
+                nc.vector.tensor_scalar(
+                    out=amp[j][:], in0=tanh_amp[j][:], scalar1=math.sqrt(0.5), scalar2=math.sqrt(0.5), op0=ALU.mult, op1=ALU.add
+                )
 
         def finish(q):
             scaled_square = {}
@@ -217,11 +245,18 @@ def tile_quantuminspiredneuralcore_pa_kernel(tc, x, amp_w, amp_b, ph_w, ph_b, ou
                     nc.vector.scalar_tensor_tensor(
                         out=result[:], in0=scaled_square[j][:], scalar=math.sqrt(0.5), in1=amp_turned[j][:], op0=ALU.add, op1=ALU.mult
                     )
+                elif q == CHUNKS - 1:
+                    for part in parts_of(j):
+                        nc.vector.tensor_tensor(
+                            out=result[:, part, :], in0=amp_turned[j][:, part, :], in1=sine[j][:, part, :], op=ALU.mult
+                        )
+                        nc.sync.dma_start(out=out_dram[:, part, j * P : (j + 1) * P], in_=result[:, part, :])
                 else:
                     nc.vector.scalar_tensor_tensor(
                         out=result[:], in0=amp_turned[j][:], scalar=math.sqrt(0.5), in1=sine[j][:], op0=ALU.mult, op1=ALU.mult
                     )
-                nc.sync.dma_start(out=out_dram[:, :, j * P : (j + 1) * P], in_=result[:])
+                if q < CHUNKS - 1:
+                    nc.sync.dma_start(out=out_dram[:, :, j * P : (j + 1) * P], in_=result[:])
 
         prepare_weights("ph", 0, scalar_passes=(1,))
 
@@ -233,6 +268,7 @@ def tile_quantuminspiredneuralcore_pa_kernel(tc, x, amp_w, amp_b, ph_w, ph_b, ou
             for g in range(PASSES):
                 for u in range(2):
                     nc.tensor.transpose(out=x_t[:, g, u, :], in_=words[:, g, u, :], identity=ident_f32[:])
+            keep_warm(1)
             x_grouped = keep.tile([P, PASSES * P * PACK], BF16, name="x_grouped%d" % i, align_bytes=64)
             nc.scalar.copy(
                 out=x_grouped[:].bitcast(F32).rearrange("p (g r u) -> p g r u", g=PASSES, u=2),
@@ -248,6 +284,7 @@ def tile_quantuminspiredneuralcore_pa_kernel(tc, x, amp_w, amp_b, ph_w, ph_b, ou
 
         bias_ps = psum_turned.tile([P, P], BF16, name="bias_ps", tag="amp")
         nc.tensor.transpose(out=bias_ps[:], in_=bias_rows[:], identity=ident_bf16[:])
+        keep_warm(WARM_UP_LAST)
         amp_bias_half = keep.tile([P, FEATURE_TILES], F32)
         nc.vector.tensor_scalar(
             out=amp_bias_half[:], in0=bias_ps[:, 0:FEATURE_TILES], scalar1=0.5, scalar2=None, op0=ALU.mult
@@ -263,16 +300,18 @@ def tile_quantuminspiredneuralcore_pa_kernel(tc, x, amp_w, amp_b, ph_w, ph_b, ou
                 multiply("amp", k)
                 squash(k)
                 for j in tiles_of(k):
-                    tanh_ph_turned[j] = turn(tanh_ph[j], "ph")
+                    tanh_ph_turned[j] = turn(tanh_ph[j], psum_turned, "ph")
                 wave(k)
             if k >= 1:
                 for j in tiles_of(k - 1):
                     if k == CHUNKS:
-                        amp_turned[j] = turn_plus_one(tanh_amp[j], psum_z, "z")
+                        amp_turned[j] = turn(amp[j], psum_z, "z")
                     else:
                         amp_turned[j] = turn_plus_one(tanh_amp[j], psum_turned, "amp")
             if k + 1 < CHUNKS:
                 prepare_weights("ph", k + 1)
                 prepare_weights("amp", k + 1)
+            if k == CHUNKS - 1:
+                scale_amp(k)
             if k >= 1:
                 finish(k - 1)

@@ -110,30 +110,33 @@ def tile_quantuminspiredneuralcore_pa_kernel(tc, x, amp_w, amp_b, ph_w, ph_b, ou
         w_codes = {}
         w_scales = {}
 
-        def prepare_weights(m, q, scalar_passes=()):
-            grouped = grouped_pool.tile([P, PASSES, CHUNK, PACK], BF16, name="grouped", align_bytes=64)
+        w_grouped = {}
+
+        def regroup_weights(m, q, g, copy, cols=slice(0, CHUNK)):
+            if (m, q) not in w_grouped:
+                w_grouped[(m, q)] = grouped_pool.tile([P, PASSES, CHUNK, PACK], BF16, name="grouped", align_bytes=64)
+            copy(
+                out=w_grouped[(m, q)][:, g, cols, :].rearrange("p (c i) t -> p c t i", i=4),
+                in_=raw[(m, q)][:, g, :, cols].rearrange("p t (c i) -> p c t i", i=4),
+            )
+
+        def quantise_weights(m, q):
             codes = quantised.tile([P, PASSES * CHUNK], U32, name="codes", align_bytes=64)
             scales = quantised.tile([P, PASSES * CHUNK], U8, name="scales", align_bytes=64)
-            for g in range(PASSES):
-                if g in scalar_passes:
-                    nc.scalar.copy(
-                        out=grouped[:, g].rearrange("p (c i) t -> p c t i", i=4),
-                        in_=raw[(m, q)][:, g].rearrange("p t (c i) -> p c t i", i=4),
-                    )
-                else:
-                    nc.vector.tensor_copy(
-                        out=grouped[:, g].rearrange("p (c i) t -> p c t i", i=4),
-                        in_=raw[(m, q)][:, g].rearrange("p t (c i) -> p c t i", i=4),
-                    )
             for g in range(PASSES):
                 cols = slice(g * CHUNK, (g + 1) * CHUNK)
                 nc.vector.quantize_mx(
                     out=codes[:, cols].bitcast(FP8X4),
                     scales=scales[:, cols],
-                    in_=grouped[:, g].rearrange("p n t -> p (n t)"),
+                    in_=w_grouped[(m, q)][:, g].rearrange("p n t -> p (n t)"),
                 )
             w_codes[(m, q)] = codes
             w_scales[(m, q)] = scales
+
+        def prepare_weights(m, q):
+            for g in range(PASSES):
+                regroup_weights(m, q, g, nc.vector.tensor_copy)
+            quantise_weights(m, q)
 
         def tiles_of(q):
             return range(q * TILES_PER_CHUNK, (q + 1) * TILES_PER_CHUNK)
@@ -258,7 +261,9 @@ def tile_quantuminspiredneuralcore_pa_kernel(tc, x, amp_w, amp_b, ph_w, ph_b, ou
                 if q < CHUNKS - 1:
                     nc.sync.dma_start(out=out_dram[:, :, j * P : (j + 1) * P], in_=result[:])
 
-        prepare_weights("ph", 0, scalar_passes=(1,))
+        regroup_weights("ph", 0, 0, nc.vector.tensor_copy)
+        regroup_weights("ph", 0, 1, nc.scalar.copy)
+        quantise_weights("ph", 0)
 
         x_codes = keep.tile([P, PASSES * TOKENS], U32, align_bytes=64)
         x_scales = keep.tile([P, PASSES * TOKENS], U8, align_bytes=64)
@@ -281,6 +286,8 @@ def tile_quantuminspiredneuralcore_pa_kernel(tc, x, amp_w, amp_b, ph_w, ph_b, ou
                     scales=x_scales[:, first : first + P],
                     in_=x_grouped[:, g * P * PACK : (g + 1) * P * PACK],
                 )
+            if 1 <= i <= TILES_PER_CHUNK:
+                regroup_weights("amp", 0, 0, nc.vector.tensor_copy, cols=slice((i - 1) * P, i * P))
 
         bias_ps = psum_turned.tile([P, P], BF16, name="bias_ps", tag="amp")
         nc.tensor.transpose(out=bias_ps[:], in_=bias_rows[:], identity=ident_bf16[:])
@@ -292,7 +299,8 @@ def tile_quantuminspiredneuralcore_pa_kernel(tc, x, amp_w, amp_b, ph_w, ph_b, ou
         ph_bias = keep.tile([P, FEATURE_TILES], F32)
         nc.vector.tensor_copy(out=ph_bias[:], in_=bias_ps[:, FEATURE_TILES : 2 * FEATURE_TILES])
 
-        prepare_weights("amp", 0, scalar_passes=(1,))
+        regroup_weights("amp", 0, 1, nc.scalar.copy)
+        quantise_weights("amp", 0)
 
         for k in range(CHUNKS + 1):
             if k < CHUNKS:

@@ -27,6 +27,7 @@ TILES_PER_CHUNK = CHUNK // P
 
 HALF_ANGLE_TILES = (1, 3, 5)
 
+RUN = 8
 WARM_UP_FIRST = 6
 WARM_UP_LAST = 2
 
@@ -116,8 +117,8 @@ def tile_quantuminspiredneuralcore_pa_kernel(tc, x, amp_w, amp_b, ph_w, ph_b, ou
             if (m, q) not in w_grouped:
                 w_grouped[(m, q)] = grouped_pool.tile([P, PASSES, CHUNK, PACK], BF16, name="grouped", align_bytes=64)
             copy(
-                out=w_grouped[(m, q)][:, g, cols, :].rearrange("p (c i) t -> p c t i", i=4),
-                in_=raw[(m, q)][:, g, :, cols].rearrange("p t (c i) -> p c t i", i=4),
+                out=w_grouped[(m, q)][:, g, cols, :].rearrange("p (c i) t -> p c t i", i=RUN),
+                in_=raw[(m, q)][:, g, :, cols].rearrange("p t (c i) -> p c t i", i=RUN),
             )
 
         def quantise_weights(m, q):

@@ -28,7 +28,7 @@ TILES_PER_CHUNK = CHUNK // P
 HALF_ANGLE_TILES = (1, 3, 5)
 
 RUN = 8
-WARM_UP_FIRST = 6
+WARM_UP_FIRST = 5
 WARM_UP_LAST = 2
 
 FLOPS = 2 * TOKENS * K * 2 * FEATURES
@@ -91,18 +91,19 @@ def tile_quantuminspiredneuralcore_pa_kernel(tc, x, amp_w, amp_b, ph_w, ph_b, ou
 
         raw = {}
 
-        def load_weights(m, q):
-            raw_tile = raw_pool.tile([P, PASSES, PACK, CHUNK], BF16, name="raw_tile")
-            for g in range(PASSES):
-                nc.sync.dma_start(out=raw_tile[:, g], in_=weights_dram[m][g, :, :, q * CHUNK : (q + 1) * CHUNK])
-            raw[(m, q)] = raw_tile
+        def load_weights(m, q, passes=range(PASSES)):
+            if (m, q) not in raw:
+                raw[(m, q)] = raw_pool.tile([P, PASSES, PACK, CHUNK], BF16, name="raw_tile")
+            for g in passes:
+                nc.sync.dma_start(out=raw[(m, q)][:, g], in_=weights_dram[m][g, :, :, q * CHUNK : (q + 1) * CHUNK])
 
-        load_weights("ph", 0)
+        load_weights("ph", 0, (0,))
         x_rows = []
         for i in range(TOKEN_TILES):
             x_tile = keep.tile([P, K], BF16, name="x_tile%d" % i)
             nc.sync.dma_start(out=x_tile[:], in_=x_rows_dram[i * P : (i + 1) * P, :])
             x_rows.append(x_tile)
+        load_weights("ph", 0, (1,))
         load_weights("amp", 0)
         for q in range(1, CHUNKS):
             load_weights("ph", q)
@@ -121,18 +122,19 @@ def tile_quantuminspiredneuralcore_pa_kernel(tc, x, amp_w, amp_b, ph_w, ph_b, ou
                 in_=raw[(m, q)][:, g, :, cols].rearrange("p t (c i) -> p c t i", i=RUN),
             )
 
-        def quantise_weights(m, q):
-            codes = quantised.tile([P, PASSES * CHUNK], U32, name="codes", align_bytes=64)
-            scales = quantised.tile([P, PASSES * CHUNK], U8, name="scales", align_bytes=64)
-            for g in range(PASSES):
+        def quantise_weights(m, q, passes=range(PASSES)):
+            if (m, q) not in w_codes:
+                w_codes[(m, q)] = quantised.tile([P, PASSES * CHUNK], U32, name="codes", align_bytes=64)
+                w_scales[(m, q)] = quantised.tile([P, PASSES * CHUNK], U8, name="scales", align_bytes=64)
+            codes = w_codes[(m, q)]
+            scales = w_scales[(m, q)]
+            for g in passes:
                 cols = slice(g * CHUNK, (g + 1) * CHUNK)
                 nc.vector.quantize_mx(
                     out=codes[:, cols].bitcast(FP8X4),
                     scales=scales[:, cols],
                     in_=w_grouped[(m, q)][:, g].rearrange("p n t -> p (n t)"),
                 )
-            w_codes[(m, q)] = codes
-            w_scales[(m, q)] = scales
 
         def prepare_weights(m, q):
             for g in range(PASSES):
@@ -263,8 +265,7 @@ def tile_quantuminspiredneuralcore_pa_kernel(tc, x, amp_w, amp_b, ph_w, ph_b, ou
                     nc.sync.dma_start(out=out_dram[:, :, j * P : (j + 1) * P], in_=result[:])
 
         regroup_weights("ph", 0, 0, nc.vector.tensor_copy)
-        regroup_weights("ph", 0, 1, nc.scalar.copy)
-        quantise_weights("ph", 0)
+        quantise_weights("ph", 0, (0,))
 
         x_codes = keep.tile([P, PASSES * TOKENS], U32, align_bytes=64)
         x_scales = keep.tile([P, PASSES * TOKENS], U8, align_bytes=64)
@@ -274,7 +275,6 @@ def tile_quantuminspiredneuralcore_pa_kernel(tc, x, amp_w, amp_b, ph_w, ph_b, ou
             for g in range(PASSES):
                 for u in range(2):
                     nc.tensor.transpose(out=x_t[:, g, u, :], in_=words[:, g, u, :], identity=ident_f32[:])
-            keep_warm(1)
             x_grouped = keep.tile([P, PASSES * P * PACK], BF16, name="x_grouped%d" % i, align_bytes=64)
             nc.scalar.copy(
                 out=x_grouped[:].bitcast(F32).rearrange("p (g r u) -> p g r u", g=PASSES, u=2),
@@ -287,8 +287,10 @@ def tile_quantuminspiredneuralcore_pa_kernel(tc, x, amp_w, amp_b, ph_w, ph_b, ou
                     scales=x_scales[:, first : first + P],
                     in_=x_grouped[:, g * P * PACK : (g + 1) * P * PACK],
                 )
-            if 1 <= i <= TILES_PER_CHUNK:
-                regroup_weights("amp", 0, 0, nc.vector.tensor_copy, cols=slice((i - 1) * P, i * P))
+            if i < TILES_PER_CHUNK:
+                regroup_weights("ph", 0, 1, nc.vector.tensor_copy, cols=slice(i * P, (i + 1) * P))
+            elif i == 2:
+                quantise_weights("ph", 0, (1,))
 
         bias_ps = psum_turned.tile([P, P], BF16, name="bias_ps", tag="amp")
         nc.tensor.transpose(out=bias_ps[:], in_=bias_rows[:], identity=ident_bf16[:])
@@ -300,7 +302,8 @@ def tile_quantuminspiredneuralcore_pa_kernel(tc, x, amp_w, amp_b, ph_w, ph_b, ou
         ph_bias = keep.tile([P, FEATURE_TILES], F32)
         nc.vector.tensor_copy(out=ph_bias[:], in_=bias_ps[:, FEATURE_TILES : 2 * FEATURE_TILES])
 
-        regroup_weights("amp", 0, 1, nc.scalar.copy)
+        regroup_weights("amp", 0, 0, nc.scalar.copy)
+        regroup_weights("amp", 0, 1, nc.vector.tensor_copy)
         quantise_weights("amp", 0)
 
         for k in range(CHUNKS + 1):

@@ -28,7 +28,7 @@ TILES_PER_CHUNK = CHUNK // P
 HALF_ANGLE_TILES = (1, 3, 5)
 
 RUN = 8
-WARM_UP_FIRST = 5
+WARM_UP_FIRST = 3
 WARM_UP_LAST = 2
 
 FLOPS = 2 * TOKENS * K * 2 * FEATURES
@@ -68,16 +68,10 @@ def tile_quantuminspiredneuralcore_pa_kernel(tc, x, amp_w, amp_b, ph_w, ph_b, ou
         make_identity(nc, ident_f32[:])
         ident_bf16 = keep.tile([P, P], BF16)
         make_identity(nc, ident_bf16[:])
-        neg_quarter = keep.tile([P, 1], F32)
-        nc.vector.memset(neg_quarter[:], -0.25)
         half = keep.tile([P, 1], F32)
         nc.vector.memset(half[:], 0.5)
-        half_pi = keep.tile([P, 1], F32)
-        nc.vector.tensor_scalar(out=half_pi[:], in0=half[:], scalar1=math.pi, scalar2=None, op0=ALU.mult)
         ones_f32 = keep.tile([P, P], F32)
         nc.vector.memset(ones_f32[:], 1.0)
-        eighth_pi = keep.tile([P, 1], F32)
-        nc.vector.tensor_scalar(out=eighth_pi[:], in0=half[:], scalar1=math.pi / 4.0, scalar2=None, op0=ALU.mult)
         bias_rows = keep.tile([P, P], BF16)
         nc.vector.memset(bias_rows[:], 0.0)
 
@@ -97,9 +91,10 @@ def tile_quantuminspiredneuralcore_pa_kernel(tc, x, amp_w, amp_b, ph_w, ph_b, ou
             for g in passes:
                 nc.sync.dma_start(out=raw[(m, q)][:, g], in_=weights_dram[m][g, :, :, q * CHUNK : (q + 1) * CHUNK])
 
-        load_weights("ph", 0, (0,))
         x_rows = []
         for i in range(TOKEN_TILES):
+            if i == TOKEN_TILES // 2:
+                load_weights("ph", 0, (0,))
             x_tile = keep.tile([P, K], BF16, name="x_tile%d" % i)
             nc.sync.dma_start(out=x_tile[:], in_=x_rows_dram[i * P : (i + 1) * P, :])
             x_rows.append(x_tile)
@@ -145,7 +140,7 @@ def tile_quantuminspiredneuralcore_pa_kernel(tc, x, amp_w, amp_b, ph_w, ph_b, ou
             return range(q * TILES_PER_CHUNK, (q + 1) * TILES_PER_CHUNK)
 
         def parts_of(j):
-            if j == FEATURE_TILES - 1:
+            if j >= FEATURE_TILES - TILES_PER_CHUNK:
                 return (slice(0, TOKEN_TILES // 2), slice(TOKEN_TILES // 2, TOKEN_TILES))
             return (slice(0, TOKEN_TILES),)
 
@@ -213,19 +208,19 @@ def tile_quantuminspiredneuralcore_pa_kernel(tc, x, amp_w, amp_b, ph_w, ph_b, ou
                 if j in HALF_ANGLE_TILES:
                     sine[j] = work.tile([P, TOKEN_TILES, P], F32, name="sine")
                     nc.scalar.activation(
-                        out=sine[j][:], in_=tanh_ph_turned[j][:], func=ACT.Sin, bias=eighth_pi[:, 0:1], scale=-math.pi / 2.0
+                        out=sine[j][:], in_=tanh_ph_turned[j][:], func=ACT.Sin, bias=math.pi / 8.0, scale=-math.pi / 2.0
                     )
                 else:
                     folded[j] = work.tile([P, TOKEN_TILES, P], F32, name="folded")
                     nc.scalar.activation(
-                        out=folded[j][:], in_=tanh_ph_turned[j][:], func=ACT.Abs, bias=neg_quarter[:, 0:1], scale=1.0
+                        out=folded[j][:], in_=tanh_ph_turned[j][:], func=ACT.Abs, bias=-0.25, scale=1.0
                     )
             for j in tiles_of(q):
                 if j not in HALF_ANGLE_TILES:
                     sine[j] = work.tile([P, TOKEN_TILES, P], F32, name="sine")
                     for part in parts_of(j):
                         nc.scalar.activation(
-                            out=sine[j][:, part, :], in_=folded[j][:, part, :], func=ACT.Sin, bias=half_pi[:, 0:1], scale=-math.pi
+                            out=sine[j][:, part, :], in_=folded[j][:, part, :], func=ACT.Sin, bias=math.pi / 2.0, scale=-math.pi
                         )
 
         amp = {}
@@ -237,14 +232,17 @@ def tile_quantuminspiredneuralcore_pa_kernel(tc, x, amp_w, amp_b, ph_w, ph_b, ou
                     out=amp[j][:], in0=tanh_amp[j][:], scalar1=math.sqrt(0.5), scalar2=math.sqrt(0.5), op0=ALU.mult, op1=ALU.add
                 )
 
-        def finish(q):
-            scaled_square = {}
+        scaled_square = {}
+
+        def square(q):
             for j in tiles_of(q):
                 if j in HALF_ANGLE_TILES:
                     scaled_square[j] = work.tile([P, TOKEN_TILES, P], F32, name="scaled_square")
                     nc.vector.scalar_tensor_tensor(
                         out=scaled_square[j][:], in0=sine[j][:], scalar=-math.sqrt(2.0), in1=sine[j][:], op0=ALU.mult, op1=ALU.mult
                     )
+
+        def finish(q):
             for j in tiles_of(q):
                 result = results.tile([P, TOKEN_TILES, P], F32, name="result")
                 if j in HALF_ANGLE_TILES:
@@ -265,7 +263,6 @@ def tile_quantuminspiredneuralcore_pa_kernel(tc, x, amp_w, amp_b, ph_w, ph_b, ou
                     nc.sync.dma_start(out=out_dram[:, :, j * P : (j + 1) * P], in_=result[:])
 
         regroup_weights("ph", 0, 0, nc.vector.tensor_copy)
-        quantise_weights("ph", 0, (0,))
 
         x_codes = keep.tile([P, PASSES * TOKENS], U32, align_bytes=64)
         x_scales = keep.tile([P, PASSES * TOKENS], U8, align_bytes=64)
@@ -287,9 +284,11 @@ def tile_quantuminspiredneuralcore_pa_kernel(tc, x, amp_w, amp_b, ph_w, ph_b, ou
                     scales=x_scales[:, first : first + P],
                     in_=x_grouped[:, g * P * PACK : (g + 1) * P * PACK],
                 )
-            if i < TILES_PER_CHUNK:
-                regroup_weights("ph", 0, 1, nc.vector.tensor_copy, cols=slice(i * P, (i + 1) * P))
-            elif i == 2:
+            if i == 0:
+                quantise_weights("ph", 0, (0,))
+            elif i <= TILES_PER_CHUNK:
+                regroup_weights("ph", 0, 1, nc.vector.tensor_copy, cols=slice((i - 1) * P, i * P))
+            else:
                 quantise_weights("ph", 0, (1,))
 
         bias_ps = psum_turned.tile([P, P], BF16, name="bias_ps", tag="amp")
@@ -323,6 +322,8 @@ def tile_quantuminspiredneuralcore_pa_kernel(tc, x, amp_w, amp_b, ph_w, ph_b, ou
             if k + 1 < CHUNKS:
                 prepare_weights("ph", k + 1)
                 prepare_weights("amp", k + 1)
+            if k >= 1:
+                square(k - 1)
             if k == CHUNKS - 1:
                 scale_amp(k)
             if k >= 1:

@@ -70,8 +70,10 @@ def tile_quantuminspiredneuralcore_pa_kernel(tc, x, amp_w, amp_b, ph_w, ph_b, ou
         make_identity(nc, ident_bf16[:])
         half = keep.tile([P, 1], F32)
         nc.vector.memset(half[:], 0.5)
-        ones_f32 = keep.tile([P, P], F32)
-        nc.vector.memset(ones_f32[:], 1.0)
+        ones = keep.tile([P, TOKENS], BF16)
+        nc.vector.memset(ones[:], 1.0)
+        one_share = keep.tile([P, P], BF16)
+        nc.vector.memset(one_share[:], 1.0 / P)
         bias_rows = keep.tile([P, P], BF16)
         nc.vector.memset(bias_rows[:], 0.0)
 
@@ -170,17 +172,17 @@ def tile_quantuminspiredneuralcore_pa_kernel(tc, x, amp_w, amp_b, ph_w, ph_b, ou
 
         def turn_plus_one(source, pool, tag):
             turned = pool.tile([P, TOKEN_TILES, P], F32, name="turned", tag=tag)
+            nc.tensor.matmul(
+                out=turned[:].rearrange("p i f -> p (i f)"), lhsT=one_share[:], rhs=ones[:], start=True, stop=False
+            )
             for i in range(TOKEN_TILES):
-                nc.tensor.matmul(
-                    out=turned[:, i, :], lhsT=ones_f32[:], rhs=ident_f32[:], is_transpose=True, start=True, stop=False
-                )
                 nc.tensor.matmul(
                     out=turned[:, i, :],
                     lhsT=source[:, i * P : (i + 1) * P],
                     rhs=ident_f32[:],
                     is_transpose=True,
                     start=False,
-                    stop=True,
+                    stop=(i == TOKEN_TILES - 1),
                 )
             return turned
 

@@ -170,11 +170,18 @@ def tile_quantuminspiredneuralcore_pa_kernel(tc, x, amp_w, amp_b, ph_w, ph_b, ou
                 nc.tensor.transpose(out=turned[:, i, :], in_=source[:, i * P : (i + 1) * P], identity=ident_f32[:])
             return turned
 
-        def turn_plus_one(source, pool, tag):
+        def open_with_one(pool, tag):
             turned = pool.tile([P, TOKEN_TILES, P], F32, name="turned", tag=tag)
             nc.tensor.matmul(
                 out=turned[:].rearrange("p i f -> p (i f)"), lhsT=one_share[:], rhs=ones[:], start=True, stop=False
             )
+            return turned
+
+        def open_amp(q):
+            for j in tiles_of(q):
+                amp_turned[j] = open_with_one(psum_turned, "amp")
+
+        def turn_onto(turned, source):
             for i in range(TOKEN_TILES):
                 nc.tensor.matmul(
                     out=turned[:, i, :],
@@ -184,7 +191,6 @@ def tile_quantuminspiredneuralcore_pa_kernel(tc, x, amp_w, amp_b, ph_w, ph_b, ou
                     start=False,
                     stop=(i == TOKEN_TILES - 1),
                 )
-            return turned
 
         tanh_ph = {}
         tanh_amp = {}
@@ -312,15 +318,19 @@ def tile_quantuminspiredneuralcore_pa_kernel(tc, x, amp_w, amp_b, ph_w, ph_b, ou
                 multiply("ph", k)
                 multiply("amp", k)
                 squash(k)
+                if 1 <= k < CHUNKS - 1:
+                    open_amp(k - 1)
                 for j in tiles_of(k):
                     tanh_ph_turned[j] = turn(tanh_ph[j], psum_turned, "ph")
+                if k == CHUNKS - 1:
+                    open_amp(k - 1)
                 wave(k)
             if k >= 1:
                 for j in tiles_of(k - 1):
                     if k == CHUNKS:
                         amp_turned[j] = turn(amp[j], psum_z, "z")
                     else:
-                        amp_turned[j] = turn_plus_one(tanh_amp[j], psum_turned, "amp")
+                        turn_onto(amp_turned[j], tanh_amp[j])
             if k + 1 < CHUNKS:
                 prepare_weights("ph", k + 1)
                 prepare_weights("amp", k + 1)

@@ -25,7 +25,7 @@ CHUNK = 256
 CHUNKS = FEATURES // CHUNK
 TILES_PER_CHUNK = CHUNK // P
 
-HALF_ANGLE_TILES = (1, 3, 5)
+HALF_ANGLE_TILES = (3, 5)
 
 RUN = 8
 WARM_UP_FIRST = 3
@@ -54,13 +54,17 @@ def tile_quantuminspiredneuralcore_pa_kernel(tc, x, amp_w, amp_b, ph_w, ph_b, ou
         psum_z = ctx.enter_context(tc.psum_pool(name="psum_z", bufs=2 * TILES_PER_CHUNK))
         psum_turned = ctx.enter_context(tc.psum_pool(name="psum_turned", bufs=TILES_PER_CHUNK))
 
-        idle_rows = keep.tile([P, TOKENS], BF16)
-        nc.vector.memset(idle_rows[:], 0.0)
+        bias_rows = keep.tile([P, P], BF16)
+        nc.vector.memset(bias_rows[:], 0.0)
+        half = keep.tile([P, 1], F32)
+        nc.vector.memset(half[:], 0.5)
+        ones = keep.tile([P, TOKENS], BF16)
+        nc.vector.memset(ones[:], 1.0)
         idle_ps = psum_turned.tile([P, TOKENS], F32, name="idle_ps", tag="ph")
 
         def keep_warm(count):
             for n in range(count):
-                nc.tensor.matmul(out=idle_ps[:], lhsT=idle_rows[:, 0:P], rhs=idle_rows[:], start=True, stop=True)
+                nc.tensor.matmul(out=idle_ps[:], lhsT=ones[:, 0:P], rhs=ones[:], start=True, stop=True)
 
         keep_warm(WARM_UP_FIRST)
 
@@ -68,14 +72,8 @@ def tile_quantuminspiredneuralcore_pa_kernel(tc, x, amp_w, amp_b, ph_w, ph_b, ou
         make_identity(nc, ident_f32[:])
         ident_bf16 = keep.tile([P, P], BF16)
         make_identity(nc, ident_bf16[:])
-        half = keep.tile([P, 1], F32)
-        nc.vector.memset(half[:], 0.5)
-        ones = keep.tile([P, TOKENS], BF16)
-        nc.vector.memset(ones[:], 1.0)
         one_share = keep.tile([P, P], BF16)
         nc.vector.memset(one_share[:], 1.0 / P)
-        bias_rows = keep.tile([P, P], BF16)
-        nc.vector.memset(bias_rows[:], 0.0)
 
         nc.scalar.dma_start(out=bias_rows[0:FEATURE_TILES, :], in_=amp_b.rearrange("(j f) -> j f", f=P))
         nc.scalar.dma_start(

@@ -175,9 +175,8 @@ def tile_quantuminspiredneuralcore_pa_kernel(tc, x, amp_w, amp_b, ph_w, ph_b, ou
             )
             return turned
 
-        def open_amp(q):
-            for j in tiles_of(q):
-                amp_turned[j] = open_with_one(psum_turned, "amp")
+        def open_amp(j, tag):
+            amp_turned[j] = open_with_one(psum_turned, tag)
 
         def turn_onto(turned, source):
             for i in range(TOKEN_TILES):
@@ -231,42 +230,46 @@ def tile_quantuminspiredneuralcore_pa_kernel(tc, x, amp_w, amp_b, ph_w, ph_b, ou
 
         amp = {}
 
-        def scale_amp(q):
-            for j in tiles_of(q):
-                amp[j] = work.tile([P, TOKENS], F32, name="amp")
-                nc.vector.tensor_scalar(
-                    out=amp[j][:], in0=tanh_amp[j][:], scalar1=math.sqrt(0.5), scalar2=math.sqrt(0.5), op0=ALU.mult, op1=ALU.add
-                )
+        def scale_amp(j):
+            amp[j] = work.tile([P, TOKENS], F32, name="amp")
+            nc.vector.tensor_scalar(
+                out=amp[j][:], in0=tanh_amp[j][:], scalar1=math.sqrt(0.5), scalar2=math.sqrt(0.5), op0=ALU.mult, op1=ALU.add
+            )
 
         scaled_square = {}
 
-        def square(q):
-            for j in tiles_of(q):
-                if j in HALF_ANGLE_TILES:
-                    scaled_square[j] = work.tile([P, TOKEN_TILES, P], F32, name="scaled_square")
-                    nc.vector.scalar_tensor_tensor(
-                        out=scaled_square[j][:], in0=sine[j][:], scalar=-math.sqrt(2.0), in1=sine[j][:], op0=ALU.mult, op1=ALU.mult
-                    )
+        def square(j):
+            scaled_square[j] = work.tile([P, TOKEN_TILES, P], F32, name="scaled_square")
+            nc.vector.scalar_tensor_tensor(
+                out=scaled_square[j][:], in0=sine[j][:], scalar=-math.sqrt(2.0), in1=sine[j][:], op0=ALU.mult, op1=ALU.mult
+            )
 
-        def finish(q):
-            for j in tiles_of(q):
-                result = results.tile([P, TOKEN_TILES, P], F32, name="result")
+        def finish(j):
+            result = results.tile([P, TOKEN_TILES, P], F32, name="result")
+            for part in parts_of(j):
                 if j in HALF_ANGLE_TILES:
                     nc.vector.scalar_tensor_tensor(
-                        out=result[:], in0=scaled_square[j][:], scalar=math.sqrt(0.5), in1=amp_turned[j][:], op0=ALU.add, op1=ALU.mult
+                        out=result[:, part, :],
+                        in0=scaled_square[j][:, part, :],
+                        scalar=math.sqrt(0.5),
+                        in1=amp_turned[j][:, part, :],
+                        op0=ALU.add,
+                        op1=ALU.mult,
                     )
-                elif q == CHUNKS - 1:
-                    for part in parts_of(j):
-                        nc.vector.tensor_tensor(
-                            out=result[:, part, :], in0=amp_turned[j][:, part, :], in1=sine[j][:, part, :], op=ALU.mult
-                        )
-                        nc.sync.dma_start(out=out_dram[:, part, j * P : (j + 1) * P], in_=result[:, part, :])
+                elif j in amp:
+                    nc.vector.tensor_tensor(
+                        out=result[:, part, :], in0=amp_turned[j][:, part, :], in1=sine[j][:, part, :], op=ALU.mult
+                    )
                 else:
                     nc.vector.scalar_tensor_tensor(
-                        out=result[:], in0=amp_turned[j][:], scalar=math.sqrt(0.5), in1=sine[j][:], op0=ALU.mult, op1=ALU.mult
+                        out=result[:, part, :],
+                        in0=amp_turned[j][:, part, :],
+                        scalar=math.sqrt(0.5),
+                        in1=sine[j][:, part, :],
+                        op0=ALU.mult,
+                        op1=ALU.mult,
                     )
-                if q < CHUNKS - 1:
-                    nc.sync.dma_start(out=out_dram[:, :, j * P : (j + 1) * P], in_=result[:])
+                nc.sync.dma_start(out=out_dram[:, part, j * P : (j + 1) * P], in_=result[:, part, :])
 
         regroup_weights("ph", 0, 0, nc.vector.tensor_copy)
 
@@ -311,30 +314,46 @@ def tile_quantuminspiredneuralcore_pa_kernel(tc, x, amp_w, amp_b, ph_w, ph_b, ou
         regroup_weights("amp", 0, 1, nc.vector.tensor_copy)
         quantise_weights("amp", 0)
 
-        for k in range(CHUNKS + 1):
-            if k < CHUNKS:
-                multiply("ph", k)
-                multiply("amp", k)
-                squash(k)
-                if 1 <= k < CHUNKS - 1:
-                    open_amp(k - 1)
-                for j in tiles_of(k):
+        for k in range(CHUNKS):
+            last = k == CHUNKS - 1
+            multiply("ph", k)
+            multiply("amp", k)
+            squash(k)
+            a, b = tiles_of(k)
+            if not last:
+                if k >= 1:
+                    open_amp(a - 2, "amp")
+                    open_amp(b - 2, "amp")
+                for j in (a, b):
                     tanh_ph_turned[j] = turn(tanh_ph[j], psum_turned, "ph")
-                if k == CHUNKS - 1:
-                    open_amp(k - 1)
-                wave(k)
-            if k >= 1:
-                for j in tiles_of(k - 1):
-                    if k == CHUNKS:
-                        amp_turned[j] = turn(amp[j], psum_z, "z")
-                    else:
-                        turn_onto(amp_turned[j], tanh_amp[j])
-            if k + 1 < CHUNKS:
+                if k >= 1:
+                    turn_onto(amp_turned[a - 2], tanh_amp[a - 2])
+                    turn_onto(amp_turned[b - 2], tanh_amp[b - 2])
+            else:
+                open_amp(a - 2, "ph")
+                turn_onto(amp_turned[a - 2], tanh_amp[a - 2])
+                tanh_ph_turned[a] = turn(tanh_ph[a], psum_turned, "ph")
+                tanh_ph_turned[b] = turn(tanh_ph[b], psum_turned, "amp")
+                open_amp(b - 2, "amp")
+                turn_onto(amp_turned[b - 2], tanh_amp[b - 2])
+            wave(k)
+            if not last:
                 prepare_weights("ph", k + 1)
                 prepare_weights("amp", k + 1)
-            if k >= 1:
-                square(k - 1)
-            if k == CHUNKS - 1:
-                scale_amp(k)
-            if k >= 1:
-                finish(k - 1)
+            if k >= 1 and not last:
+                for j in (a - 2, b - 2):
+                    if j in HALF_ANGLE_TILES:
+                        square(j)
+                for j in (a - 2, b - 2):
+                    finish(j)
+            if last:
+                for j in (a - 2, b - 2):
+                    if j in HALF_ANGLE_TILES:
+                        square(j)
+                for j in (a, b):
+                    scale_amp(j)
+                    finish(j - 2)
+        for j in tiles_of(CHUNKS - 1):
+            amp_turned[j] = turn(amp[j], psum_z, "z")
+        for j in tiles_of(CHUNKS - 1):
+            finish(j)

import math
from contextlib import ExitStack

import concourse.mybir as mybir
from concourse.masks import make_identity

BF16 = mybir.dt.bfloat16
F32 = mybir.dt.float32
U32 = mybir.dt.uint32
U8 = mybir.dt.uint8
FP8X4 = mybir.dt.float8_e4m3fn_x4
ACT = mybir.ActivationFunctionType
ALU = mybir.AluOpType

P = 128
PACK = 4
K_PASS = P * PACK
TOKENS = 512
K = 1024
FEATURES = 1024
PASSES = K // K_PASS
TOKEN_TILES = TOKENS // P
FEATURE_TILES = FEATURES // P
CHUNK = 256
CHUNKS = FEATURES // CHUNK
TILES_PER_CHUNK = CHUNK // P

HALF_ANGLE_TILES = (3, 5)

RUN = 8
WARM_UP_FIRST = 3
WARM_UP_LAST = 2

FLOPS = 2 * TOKENS * K * 2 * FEATURES


def tile_quantuminspiredneuralcore_pa_kernel(tc, x, amp_w, amp_b, ph_w, ph_b, out):
    nc = tc.nc
    x_rows_dram = x.flatten_outer_dims()
    weights_dram = {
        "ph": ph_w.rearrange("(g p t) n -> g p t n", g=PASSES, t=PACK),
        "amp": amp_w.rearrange("(g p t) n -> g p t n", g=PASSES, t=PACK),
    }
    out_dram = out.flatten_outer_dims().rearrange("(i p) f -> p i f", p=P)

    with ExitStack() as ctx:
        ctx.enter_context(tc.manual_schedule())
        keep = ctx.enter_context(tc.tile_pool(name="keep", bufs=1))
        raw_pool = ctx.enter_context(tc.tile_pool(name="raw", bufs=2 * CHUNKS))
        grouped_pool = ctx.enter_context(tc.tile_pool(name="grouped", bufs=3))
        quantised = ctx.enter_context(tc.tile_pool(name="quantised", bufs=2 * CHUNKS))
        work = ctx.enter_context(tc.tile_pool(name="work", bufs=3 * TILES_PER_CHUNK))
        results = ctx.enter_context(tc.tile_pool(name="results", bufs=FEATURE_TILES))
        psum_z = ctx.enter_context(tc.psum_pool(name="psum_z", bufs=2 * TILES_PER_CHUNK))
        psum_turned = ctx.enter_context(tc.psum_pool(name="psum_turned", bufs=TILES_PER_CHUNK))

        bias_rows = keep.tile([P, P], BF16)
        nc.vector.memset(bias_rows[:], 0.0)
        half = keep.tile([P, 1], F32)
        nc.vector.memset(half[:], 0.5)
        ones = keep.tile([P, TOKENS], BF16)
        nc.vector.memset(ones[:], 1.0)
        idle_ps = psum_turned.tile([P, TOKENS], F32, name="idle_ps", tag="ph")

        def keep_warm(count):
            for n in range(count):
                nc.tensor.matmul(out=idle_ps[:], lhsT=ones[:, 0:P], rhs=ones[:], start=True, stop=True)

        keep_warm(WARM_UP_FIRST)

        ident_f32 = keep.tile([P, P], F32)
        make_identity(nc, ident_f32[:])
        ident_bf16 = keep.tile([P, P], BF16)
        make_identity(nc, ident_bf16[:])
        one_share = keep.tile([P, P], BF16)
        nc.vector.memset(one_share[:], 1.0 / P)

        nc.scalar.dma_start(out=bias_rows[0:FEATURE_TILES, :], in_=amp_b.rearrange("(j f) -> j f", f=P))
        nc.scalar.dma_start(
            out=bias_rows[FEATURE_TILES : 2 * FEATURE_TILES, :], in_=ph_b.rearrange("(j f) -> j f", f=P)
        )

        warm = keep.tile([P, 1], F32)
        nc.scalar.activation(out=warm[:], in_=half[:], func=ACT.Silu)

        raw = {}

        def load_weights(m, q, passes=range(PASSES)):
            if (m, q) not in raw:
                raw[(m, q)] = raw_pool.tile([P, PASSES, PACK, CHUNK], BF16, name="raw_tile")
            for g in passes:
                nc.sync.dma_start(out=raw[(m, q)][:, g], in_=weights_dram[m][g, :, :, q * CHUNK : (q + 1) * CHUNK])

        x_rows = []
        for i in range(TOKEN_TILES):
            if i == TOKEN_TILES // 2:
                load_weights("ph", 0, (0,))
            x_tile = keep.tile([P, K], BF16, name="x_tile%d" % i)
            nc.sync.dma_start(out=x_tile[:], in_=x_rows_dram[i * P : (i + 1) * P, :])
            x_rows.append(x_tile)
        load_weights("ph", 0, (1,))
        load_weights("amp", 0)
        for q in range(1, CHUNKS):
            load_weights("ph", q)
            load_weights("amp", q)

        w_codes = {}
        w_scales = {}

        w_grouped = {}

        def regroup_weights(m, q, g, copy, cols=slice(0, CHUNK)):
            if (m, q) not in w_grouped:
                w_grouped[(m, q)] = grouped_pool.tile([P, PASSES, CHUNK, PACK], BF16, name="grouped", align_bytes=64)
            copy(
                out=w_grouped[(m, q)][:, g, cols, :].rearrange("p (c i) t -> p c t i", i=RUN),
                in_=raw[(m, q)][:, g, :, cols].rearrange("p t (c i) -> p c t i", i=RUN),
            )

        def quantise_weights(m, q, passes=range(PASSES)):
            if (m, q) not in w_codes:
                w_codes[(m, q)] = quantised.tile([P, PASSES * CHUNK], U32, name="codes", align_bytes=64)
                w_scales[(m, q)] = quantised.tile([P, PASSES * CHUNK], U8, name="scales", align_bytes=64)
            codes = w_codes[(m, q)]
            scales = w_scales[(m, q)]
            for g in passes:
                cols = slice(g * CHUNK, (g + 1) * CHUNK)
                nc.vector.quantize_mx(
                    out=codes[:, cols].bitcast(FP8X4),
                    scales=scales[:, cols],
                    in_=w_grouped[(m, q)][:, g].rearrange("p n t -> p (n t)"),
                )

        def prepare_weights(m, q):
            for g in range(PASSES):
                regroup_weights(m, q, g, nc.vector.tensor_copy)
            quantise_weights(m, q)

        def tiles_of(q):
            return range(q * TILES_PER_CHUNK, (q + 1) * TILES_PER_CHUNK)

        def parts_of(j):
            if j >= FEATURE_TILES - TILES_PER_CHUNK:
                return (slice(0, TOKEN_TILES // 2), slice(TOKEN_TILES // 2, TOKEN_TILES))
            return (slice(0, TOKEN_TILES),)

        z = {}

        def multiply(m, q):
            for jj, j in enumerate(tiles_of(q)):
                z[(m, j)] = psum_z.tile([P, TOKENS], F32, name="z")
                for g in range(PASSES):
                    w_cols = slice(g * CHUNK + jj * P, g * CHUNK + (jj + 1) * P)
                    x_cols = slice(g * TOKENS, (g + 1) * TOKENS)
                    nc.tensor.matmul_mx(
                        out=z[(m, j)][:],
                        lhsT=w_codes[(m, q)][:, w_cols].bitcast(FP8X4),
                        lhsT_scale=w_scales[(m, q)][:, w_cols],
                        rhs=x_codes[:, x_cols].bitcast(FP8X4),
                        rhs_scale=x_scales[:, x_cols],
                        start=(g == 0),
                        stop=(g == PASSES - 1),
                    )

        def turn(source, pool, tag):
            turned = pool.tile([P, TOKEN_TILES, P], F32, name="turned", tag=tag)
            for i in range(TOKEN_TILES):
                nc.tensor.transpose(out=turned[:, i, :], in_=source[:, i * P : (i + 1) * P], identity=ident_f32[:])
            return turned

        def open_with_one(pool, tag):
            turned = pool.tile([P, TOKEN_TILES, P], F32, name="turned", tag=tag)
            nc.tensor.matmul(
                out=turned[:].rearrange("p i f -> p (i f)"), lhsT=one_share[:], rhs=ones[:], start=True, stop=False
            )
            return turned

        def open_amp(j, tag):
            amp_turned[j] = open_with_one(psum_turned, tag)

        def turn_onto(turned, source):
            for i in range(TOKEN_TILES):
                nc.tensor.matmul(
                    out=turned[:, i, :],
                    lhsT=source[:, i * P : (i + 1) * P],
                    rhs=ident_f32[:],
                    is_transpose=True,
                    start=False,
                    stop=(i == TOKEN_TILES - 1),
                )

        tanh_ph = {}
        tanh_amp = {}
        tanh_ph_turned = {}
        amp_turned = {}
        sine = {}

        def squash(q):
            for j in tiles_of(q):
                tanh_ph[j] = work.tile([P, TOKENS], F32, name="tanh_ph")
                nc.scalar.activation(
                    out=tanh_ph[j][:], in_=z[("ph", j)][:], func=ACT.Tanh, bias=ph_bias[:, j : j + 1], scale=1.0
                )
            for j in tiles_of(q):
                tanh_amp[j] = work.tile([P, TOKENS], F32, name="tanh_amp")
                nc.scalar.activation(
                    out=tanh_amp[j][:], in_=z[("amp", j)][:], func=ACT.Tanh, bias=amp_bias_half[:, j : j + 1], scale=0.5
                )

        def wave(q):
            folded = {}
            for j in tiles_of(q):
                if j in HALF_ANGLE_TILES:
                    sine[j] = work.tile([P, TOKEN_TILES, P], F32, name="sine")
                    nc.scalar.activation(
                        out=sine[j][:], in_=tanh_ph_turned[j][:], func=ACT.Sin, bias=math.pi / 8.0, scale=-math.pi / 2.0
                    )
                else:
                    folded[j] = work.tile([P, TOKEN_TILES, P], F32, name="folded")
                    nc.scalar.activation(
                        out=folded[j][:], in_=tanh_ph_turned[j][:], func=ACT.Abs, bias=-0.25, scale=1.0
                    )
            for j in tiles_of(q):
                if j not in HALF_ANGLE_TILES:
                    sine[j] = work.tile([P, TOKEN_TILES, P], F32, name="sine")
                    for part in parts_of(j):
                        nc.scalar.activation(
                            out=sine[j][:, part, :], in_=folded[j][:, part, :], func=ACT.Sin, bias=math.pi / 2.0, scale=-math.pi
                        )

        amp = {}

        def scale_amp(j):
            amp[j] = work.tile([P, TOKENS], F32, name="amp")
            nc.vector.tensor_scalar(
                out=amp[j][:], in0=tanh_amp[j][:], scalar1=math.sqrt(0.5), scalar2=math.sqrt(0.5), op0=ALU.mult, op1=ALU.add
            )

        scaled_square = {}

        def square(j):
            scaled_square[j] = work.tile([P, TOKEN_TILES, P], F32, name="scaled_square")
            nc.vector.scalar_tensor_tensor(
                out=scaled_square[j][:], in0=sine[j][:], scalar=-math.sqrt(2.0), in1=sine[j][:], op0=ALU.mult, op1=ALU.mult
            )

        def finish(j):
            result = results.tile([P, TOKEN_TILES, P], F32, name="result")
            for part in parts_of(j):
                if j in HALF_ANGLE_TILES:
                    nc.vector.scalar_tensor_tensor(
                        out=result[:, part, :],
                        in0=scaled_square[j][:, part, :],
                        scalar=math.sqrt(0.5),
                        in1=amp_turned[j][:, part, :],
                        op0=ALU.add,
                        op1=ALU.mult,
                    )
                elif j in amp:
                    nc.vector.tensor_tensor(
                        out=result[:, part, :], in0=amp_turned[j][:, part, :], in1=sine[j][:, part, :], op=ALU.mult
                    )
                else:
                    nc.vector.scalar_tensor_tensor(
                        out=result[:, part, :],
                        in0=amp_turned[j][:, part, :],
                        scalar=math.sqrt(0.5),
                        in1=sine[j][:, part, :],
                        op0=ALU.mult,
                        op1=ALU.mult,
                    )
                nc.sync.dma_start(out=out_dram[:, part, j * P : (j + 1) * P], in_=result[:, part, :])

        regroup_weights("ph", 0, 0, nc.vector.tensor_copy)

        x_codes = keep.tile([P, PASSES * TOKENS], U32, align_bytes=64)
        x_scales = keep.tile([P, PASSES * TOKENS], U8, align_bytes=64)
        for i in range(TOKEN_TILES):
            words = x_rows[i][:].bitcast(F32).rearrange("r (g p u) -> r g u p", g=PASSES, u=2)
            x_t = psum_z.tile([P, PASSES, 2, P], F32, name="x_t", tag="z")
            for g in range(PASSES):
                for u in range(2):
                    nc.tensor.transpose(out=x_t[:, g, u, :], in_=words[:, g, u, :], identity=ident_f32[:])
            x_grouped = keep.tile([P, PASSES * P * PACK], BF16, name="x_grouped%d" % i, align_bytes=64)
            nc.scalar.copy(
                out=x_grouped[:].bitcast(F32).rearrange("p (g r u) -> p g r u", g=PASSES, u=2),
                in_=x_t[:].rearrange("p g u r -> p g r u"),
            )
            for g in range(PASSES):
                first = g * TOKENS + i * P
                nc.vector.quantize_mx(
                    out=x_codes[:, first : first + P].bitcast(FP8X4),
                    scales=x_scales[:, first : first + P],
                    in_=x_grouped[:, g * P * PACK : (g + 1) * P * PACK],
                )
            if i == 0:
                quantise_weights("ph", 0, (0,))
            elif i <= TILES_PER_CHUNK:
                regroup_weights("ph", 0, 1, nc.vector.tensor_copy, cols=slice((i - 1) * P, i * P))
            else:
                quantise_weights("ph", 0, (1,))

        bias_ps = psum_turned.tile([P, P], BF16, name="bias_ps", tag="amp")
        nc.tensor.transpose(out=bias_ps[:], in_=bias_rows[:], identity=ident_bf16[:])
        keep_warm(WARM_UP_LAST)
        amp_bias_half = keep.tile([P, FEATURE_TILES], F32)
        nc.vector.tensor_scalar(
            out=amp_bias_half[:], in0=bias_ps[:, 0:FEATURE_TILES], scalar1=0.5, scalar2=None, op0=ALU.mult
        )
        ph_bias = keep.tile([P, FEATURE_TILES], F32)
        nc.vector.tensor_copy(out=ph_bias[:], in_=bias_ps[:, FEATURE_TILES : 2 * FEATURE_TILES])

        regroup_weights("amp", 0, 0, nc.scalar.copy)
        regroup_weights("amp", 0, 1, nc.vector.tensor_copy)
        quantise_weights("amp", 0)

        for k in range(CHUNKS):
            last = k == CHUNKS - 1
            multiply("ph", k)
            multiply("amp", k)
            squash(k)
            a, b = tiles_of(k)
            if not last:
                if k >= 1:
                    open_amp(a - 2, "amp")
                    open_amp(b - 2, "amp")
                for j in (a, b):
                    tanh_ph_turned[j] = turn(tanh_ph[j], psum_turned, "ph")
                if k >= 1:
                    turn_onto(amp_turned[a - 2], tanh_amp[a - 2])
                    turn_onto(amp_turned[b - 2], tanh_amp[b - 2])
            else:
                open_amp(a - 2, "ph")
                turn_onto(amp_turned[a - 2], tanh_amp[a - 2])
                tanh_ph_turned[a] = turn(tanh_ph[a], psum_turned, "ph")
                tanh_ph_turned[b] = turn(tanh_ph[b], psum_turned, "amp")
                open_amp(b - 2, "amp")
                turn_onto(amp_turned[b - 2], tanh_amp[b - 2])
            wave(k)
            if not last:
                prepare_weights("ph", k + 1)
                prepare_weights("amp", k + 1)
            if k >= 1 and not last:
                for j in (a - 2, b - 2):
                    if j in HALF_ANGLE_TILES:
                        square(j)
                for j in (a - 2, b - 2):
                    finish(j)
            if last:
                for j in (a - 2, b - 2):
                    if j in HALF_ANGLE_TILES:
                        square(j)
                for j in (a, b):
                    scale_amp(j)
                    finish(j - 2)
        for j in tiles_of(CHUNKS - 1):
            amp_turned[j] = turn(amp[j], psum_z, "z")
        for j in tiles_of(CHUNKS - 1):
            finish(j)
